import numpy as np
import ml_dtypes

BF16 = ml_dtypes.bfloat16


def bf(x):
    return np.asarray(x, np.float32).astype(BF16)


def f32(x):
    return np.asarray(x, np.float32)


def f64(x):
    return np.asarray(x).astype(np.float64)


def striped(idx):
    return np.tile(idx.reshape(-1, 16).T, (8, 1))


C, S, N, R, Q = 512, 4096, 2048, 64, 64


def setup_inputs():
    return {"emb": f32(np.random.standard_normal((C, S))), "row": f32(np.random.choice(R, (1, N))), "col": f32(np.random.choice(Q, (1, N))), "mask": f32(np.random.random((1, N)) < 0.5), "row_vec": f32(0.02 * np.random.standard_normal((C, 1))), "col_vec": f32(0.02 * np.random.standard_normal((C, 1))), "offs": striped(np.random.permutation(np.tile(np.arange(S), 2))[:N])}


def reference(emb, row, col, mask, row_vec, col_vec, offs):
    idx = offs[:16].T.reshape(-1)
    pos = (f64(row) + 1.0) * f64(row_vec) + (f64(col) + 1.0) * f64(col_vec)
    return f64(emb)[:, idx] + f64(mask) * pos

@@ -1,0 +1,57 @@
+import concourse.mybir as mybir
+
+F32 = mybir.dt.float32
+U16 = mybir.dt.uint16
+ADD = mybir.AluOpType.add
+MULT = mybir.AluOpType.mult
+COPY = mybir.ActivationFunctionType.Copy
+
+P = 128
+C, S, N = 512, 4096, 2048
+BLOCKS = C // P
+PIECE = 512
+PIECES = N // PIECE
+
+FLOPS = 4 * C * N
+BYTES = 4 * (2 * C * N + 3 * N + 2 * C) + 2 * P * (N // 16)
+
+
+def tile_gridembedding_kernel(tc, emb, row, col, mask, row_vec, col_vec, offs, out):
+    nc = tc.nc
+    with (
+        tc.tile_pool(name="held", bufs=1) as held,
+        tc.tile_pool(name="blocks", bufs=BLOCKS) as blocks,
+        tc.psum_pool(name="psum", bufs=4) as psum,
+    ):
+        offsets = held.tile([P, N // 16], U16, name="offsets")
+        nc.sync.dma_start(offsets[:], offs)
+
+        grid = held.tile([2, N], F32, name="grid")
+        inside = held.tile([2, N], F32, name="inside")
+        vecs = held.tile([2, C], F32, name="vecs")
+        nc.scalar.dma_start(grid[0:1, :], row)
+        nc.scalar.dma_start(grid[1:2, :], col)
+        nc.scalar.dma_start(inside[:], mask.broadcast_to([2, N]))
+        nc.scalar.dma_start(vecs[0:1, :], row_vec.rearrange("c o -> o c"))
+        nc.scalar.dma_start(vecs[1:2, :], col_vec.rearrange("c o -> o c"))
+
+        tables = [held.tile([P, S], F32, name=f"table{b}") for b in range(BLOCKS)]
+        for b in range(BLOCKS):
+            nc.sync.dma_start(tables[b][:], emb[b * P : (b + 1) * P, :])
+
+        ab = held.tile([2, N], F32, name="ab")
+        for q in range(PIECES):
+            piece = slice(q * PIECE, (q + 1) * PIECE)
+            nc.vector.scalar_tensor_tensor(ab[:, piece], grid[:, piece], 1.0, inside[:, piece], ADD, MULT)
+
+        for b in range(BLOCKS):
+            pos = blocks.tile([P, N], F32, name="pos")
+            summed = blocks.tile([P, N], F32, name="summed")
+            for q in range(PIECES):
+                piece = slice(q * PIECE, (q + 1) * PIECE)
+                pos_bank = psum.tile([P, PIECE], F32, name="pos_bank")
+                nc.tensor.matmul(pos_bank[:], vecs[:, b * P : (b + 1) * P], ab[:, piece], start=True, stop=True)
+                nc.scalar.activation(pos[:, piece], pos_bank[:], COPY)
+                looked_up = tables[b][:].indirect(offsets[:, q * (PIECE // 16) : (q + 1) * (PIECE // 16)])
+                nc.vector.tensor_tensor(summed[:, piece], looked_up, pos[:, piece], ADD)
+            nc.sync.dma_start(out[b * P : (b + 1) * P, :], summed[:])

@@ -1,8 +1,10 @@
 import concourse.mybir as mybir
 
 F32 = mybir.dt.float32
+BF16 = mybir.dt.bfloat16
 U16 = mybir.dt.uint16
 ADD = mybir.AluOpType.add
+SUBTRACT = mybir.AluOpType.subtract
 MULT = mybir.AluOpType.mult
 COPY = mybir.ActivationFunctionType.Copy
 
@@ -11,6 +13,8 @@ C, S, N = 512, 4096, 2048
 BLOCKS = C // P
 PIECE = 512
 PIECES = N // PIECE
+TERMS = 3
+ROWS = 2 * TERMS
 
 FLOPS = 4 * C * N
 BYTES = 4 * (2 * C * N + 3 * N + 2 * C) + 2 * P * (N // 16)
@@ -26,20 +30,30 @@ def tile_gridembedding_kernel(tc, emb, row, col, mask, row_vec, col_vec, offs, o
         offsets = held.tile([P, N // 16], U16, name="offsets")
         nc.sync.dma_start(offsets[:], offs)
 
-        grid = held.tile([2, N], F32, name="grid")
-        inside = held.tile([2, N], F32, name="inside")
-        vecs = held.tile([2, C], F32, name="vecs")
-        nc.scalar.dma_start(grid[0:1, :], row)
-        nc.scalar.dma_start(grid[1:2, :], col)
-        nc.scalar.dma_start(inside[:], mask.broadcast_to([2, N]))
-        nc.scalar.dma_start(vecs[0:1, :], row_vec.rearrange("c o -> o c"))
-        nc.scalar.dma_start(vecs[1:2, :], col_vec.rearrange("c o -> o c"))
+        vecs = held.tile([ROWS, C], F32, name="vecs")
+        grid = held.tile([ROWS, N], F32, name="grid")
+        inside = held.tile([ROWS, N], F32, name="inside")
+        vecs_by_term = vecs[:].rearrange("(t w) c -> t w c", w=2)
+        grid_by_term = grid[:].rearrange("(t w) n -> t w n", w=2)
+        nc.sync.dma_start(vecs_by_term[:, 0, :], row_vec.rearrange("c o -> o c").broadcast_to([TERMS, C]))
+        nc.sync.dma_start(vecs_by_term[:, 1, :], col_vec.rearrange("c o -> o c").broadcast_to([TERMS, C]))
+        nc.sync.dma_start(grid_by_term[:, 0, :], row.broadcast_to([TERMS, N]))
+        nc.sync.dma_start(grid_by_term[:, 1, :], col.broadcast_to([TERMS, N]))
+        nc.sync.dma_start(inside[:], mask.broadcast_to([ROWS, N]))
 
         tables = [held.tile([P, S], F32, name=f"table{b}") for b in range(BLOCKS)]
         for b in range(BLOCKS):
             nc.sync.dma_start(tables[b][:], emb[b * P : (b + 1) * P, :])
 
-        ab = held.tile([2, N], F32, name="ab")
+        terms = held.tile([ROWS, C], BF16, name="terms")
+        rest = held.tile([4, C], F32, name="rest")
+        nc.vector.tensor_copy(terms[:], vecs[:])
+        nc.vector.tensor_tensor(rest[0:4, :], vecs[0:4, :], terms[0:4, :], SUBTRACT)
+        nc.vector.tensor_copy(terms[0:4, :], rest[0:4, :])
+        nc.vector.tensor_tensor(rest[0:2, :], rest[0:2, :], terms[0:2, :], SUBTRACT)
+        nc.vector.tensor_copy(terms[0:2, :], rest[0:2, :])
+
+        ab = held.tile([ROWS, N], BF16, name="ab")
         for q in range(PIECES):
             piece = slice(q * PIECE, (q + 1) * PIECE)
             nc.vector.scalar_tensor_tensor(ab[:, piece], grid[:, piece], 1.0, inside[:, piece], ADD, MULT)
@@ -50,7 +64,7 @@ def tile_gridembedding_kernel(tc, emb, row, col, mask, row_vec, col_vec, offs, o
             for q in range(PIECES):
                 piece = slice(q * PIECE, (q + 1) * PIECE)
                 pos_bank = psum.tile([P, PIECE], F32, name="pos_bank")
-                nc.tensor.matmul(pos_bank[:], vecs[:, b * P : (b + 1) * P], ab[:, piece], start=True, stop=True)
+                nc.tensor.matmul(pos_bank[:], terms[:, b * P : (b + 1) * P], ab[:, piece], start=True, stop=True)
                 nc.scalar.activation(pos[:, piece], pos_bank[:], COPY)
                 looked_up = tables[b][:].indirect(offsets[:, q * (PIECE // 16) : (q + 1) * (PIECE // 16)])
                 nc.vector.tensor_tensor(summed[:, piece], looked_up, pos[:, piece], ADD)

@@ -13,8 +13,8 @@ C, S, N = 512, 4096, 2048
 BLOCKS = C // P
 PIECE = 512
 PIECES = N // PIECE
-TERMS = 3
-ROWS = 2 * TERMS
+COPIES = 4
+ROWS = 2 * COPIES
 
 FLOPS = 4 * C * N
 BYTES = 4 * (2 * C * N + 3 * N + 2 * C) + 2 * P * (N // 16)
@@ -35,10 +35,10 @@ def tile_gridembedding_kernel(tc, emb, row, col, mask, row_vec, col_vec, offs, o
         inside = held.tile([ROWS, N], F32, name="inside")
         vecs_by_term = vecs[:].rearrange("(t w) c -> t w c", w=2)
         grid_by_term = grid[:].rearrange("(t w) n -> t w n", w=2)
-        nc.sync.dma_start(vecs_by_term[:, 0, :], row_vec.rearrange("c o -> o c").broadcast_to([TERMS, C]))
-        nc.sync.dma_start(vecs_by_term[:, 1, :], col_vec.rearrange("c o -> o c").broadcast_to([TERMS, C]))
-        nc.sync.dma_start(grid_by_term[:, 0, :], row.broadcast_to([TERMS, N]))
-        nc.sync.dma_start(grid_by_term[:, 1, :], col.broadcast_to([TERMS, N]))
+        nc.sync.dma_start(vecs_by_term[:, 0, :], row_vec.rearrange("c o -> o c").broadcast_to([COPIES, C]))
+        nc.sync.dma_start(vecs_by_term[:, 1, :], col_vec.rearrange("c o -> o c").broadcast_to([COPIES, C]))
+        nc.sync.dma_start(grid_by_term[:, 0, :], row.broadcast_to([COPIES, N]))
+        nc.sync.dma_start(grid_by_term[:, 1, :], col.broadcast_to([COPIES, N]))
         nc.sync.dma_start(inside[:], mask.broadcast_to([ROWS, N]))
 
         tables = [held.tile([P, S], F32, name=f"table{b}") for b in range(BLOCKS)]
@@ -47,7 +47,8 @@ def tile_gridembedding_kernel(tc, emb, row, col, mask, row_vec, col_vec, offs, o
 
         terms = held.tile([ROWS, C], BF16, name="terms")
         rest = held.tile([4, C], F32, name="rest")
-        nc.vector.tensor_copy(terms[:], vecs[:])
+        nc.gpsimd.memset(terms[:], 0.0)
+        nc.vector.tensor_copy(terms[0:6, :], vecs[0:6, :])
         nc.vector.tensor_tensor(rest[0:4, :], vecs[0:4, :], terms[0:4, :], SUBTRACT)
         nc.vector.tensor_copy(terms[0:4, :], rest[0:4, :])
         nc.vector.tensor_tensor(rest[0:2, :], rest[0:2, :], terms[0:2, :], SUBTRACT)
@@ -68,4 +69,7 @@ def tile_gridembedding_kernel(tc, emb, row, col, mask, row_vec, col_vec, offs, o
                 nc.scalar.activation(pos[:, piece], pos_bank[:], COPY)
                 looked_up = tables[b][:].indirect(offsets[:, q * (PIECE // 16) : (q + 1) * (PIECE // 16)])
                 nc.vector.tensor_tensor(summed[:, piece], looked_up, pos[:, piece], ADD)
-            nc.sync.dma_start(out[b * P : (b + 1) * P, :], summed[:])
+                if b == BLOCKS - 1:
+                    nc.sync.dma_start(out[b * P : (b + 1) * P, piece], summed[:, piece])
+            if b < BLOCKS - 1:
+                nc.sync.dma_start(out[b * P : (b + 1) * P, :], summed[:])

@@ -11,7 +11,9 @@ COPY = mybir.ActivationFunctionType.Copy
 P = 128
 C, S, N = 512, 4096, 2048
 BLOCKS = C // P
-PIECE = 512
+BANK = 512
+BANKS = N // BANK
+PIECE = 1024
 PIECES = N // PIECE
 COPIES = 4
 ROWS = 2 * COPIES
@@ -55,18 +57,20 @@ def tile_gridembedding_kernel(tc, emb, row, col, mask, row_vec, col_vec, offs, o
         nc.vector.tensor_copy(terms[0:2, :], rest[0:2, :])
 
         ab = held.tile([ROWS, N], BF16, name="ab")
-        for q in range(PIECES):
-            piece = slice(q * PIECE, (q + 1) * PIECE)
-            nc.vector.scalar_tensor_tensor(ab[:, piece], grid[:, piece], 1.0, inside[:, piece], ADD, MULT)
+        for k in range(BANKS):
+            bank = slice(k * BANK, (k + 1) * BANK)
+            nc.vector.scalar_tensor_tensor(ab[:, bank], grid[:, bank], 1.0, inside[:, bank], ADD, MULT)
 
         for b in range(BLOCKS):
             pos = blocks.tile([P, N], F32, name="pos")
             summed = blocks.tile([P, N], F32, name="summed")
+            for k in range(BANKS):
+                bank = slice(k * BANK, (k + 1) * BANK)
+                pos_bank = psum.tile([P, BANK], F32, name="pos_bank")
+                nc.tensor.matmul(pos_bank[:], terms[:, b * P : (b + 1) * P], ab[:, bank], start=True, stop=True)
+                nc.scalar.activation(pos[:, bank], pos_bank[:], COPY)
             for q in range(PIECES):
                 piece = slice(q * PIECE, (q + 1) * PIECE)
-                pos_bank = psum.tile([P, PIECE], F32, name="pos_bank")
-                nc.tensor.matmul(pos_bank[:], terms[:, b * P : (b + 1) * P], ab[:, piece], start=True, stop=True)
-                nc.scalar.activation(pos[:, piece], pos_bank[:], COPY)
                 looked_up = tables[b][:].indirect(offsets[:, q * (PIECE // 16) : (q + 1) * (PIECE // 16)])
                 nc.vector.tensor_tensor(summed[:, piece], looked_up, pos[:, piece], ADD)
                 if b == BLOCKS - 1:

@@ -13,7 +13,7 @@ C, S, N = 512, 4096, 2048
 BLOCKS = C // P
 BANK = 512
 BANKS = N // BANK
-PIECE = 1024
+PIECE = 512
 PIECES = N // PIECE
 COPIES = 4
 ROWS = 2 * COPIES
@@ -47,19 +47,23 @@ def tile_gridembedding_kernel(tc, emb, row, col, mask, row_vec, col_vec, offs, o
         for b in range(BLOCKS):
             nc.sync.dma_start(tables[b][:], emb[b * P : (b + 1) * P, :])
 
+        ab = held.tile([ROWS, N], BF16, name="ab")
+
+        def make_ab(k):
+            bank = slice(k * BANK, (k + 1) * BANK)
+            nc.vector.scalar_tensor_tensor(ab[:, bank], grid[:, bank], 1.0, inside[:, bank], ADD, MULT)
+
         terms = held.tile([ROWS, C], BF16, name="terms")
         rest = held.tile([4, C], F32, name="rest")
         nc.gpsimd.memset(terms[:], 0.0)
         nc.vector.tensor_copy(terms[0:6, :], vecs[0:6, :])
+        make_ab(0)
         nc.vector.tensor_tensor(rest[0:4, :], vecs[0:4, :], terms[0:4, :], SUBTRACT)
+        make_ab(1)
         nc.vector.tensor_copy(terms[0:4, :], rest[0:4, :])
-        nc.vector.tensor_tensor(rest[0:2, :], rest[0:2, :], terms[0:2, :], SUBTRACT)
-        nc.vector.tensor_copy(terms[0:2, :], rest[0:2, :])
-
-        ab = held.tile([ROWS, N], BF16, name="ab")
-        for k in range(BANKS):
-            bank = slice(k * BANK, (k + 1) * BANK)
-            nc.vector.scalar_tensor_tensor(ab[:, bank], grid[:, bank], 1.0, inside[:, bank], ADD, MULT)
+        make_ab(2)
+        nc.vector.tensor_tensor(terms[0:2, :], rest[0:2, :], terms[0:2, :], SUBTRACT)
+        make_ab(3)
 
         for b in range(BLOCKS):
             pos = blocks.tile([P, N], F32, name="pos")

@@ -13,8 +13,6 @@ C, S, N = 512, 4096, 2048
 BLOCKS = C // P
 BANK = 512
 BANKS = N // BANK
-PIECE = 512
-PIECES = N // PIECE
 COPIES = 4
 ROWS = 2 * COPIES
 
@@ -73,9 +71,10 @@ def tile_gridembedding_kernel(tc, emb, row, col, mask, row_vec, col_vec, offs, o
                 pos_bank = psum.tile([P, BANK], F32, name="pos_bank")
                 nc.tensor.matmul(pos_bank[:], terms[:, b * P : (b + 1) * P], ab[:, bank], start=True, stop=True)
                 nc.scalar.activation(pos[:, bank], pos_bank[:], COPY)
-            for q in range(PIECES):
-                piece = slice(q * PIECE, (q + 1) * PIECE)
-                looked_up = tables[b][:].indirect(offsets[:, q * (PIECE // 16) : (q + 1) * (PIECE // 16)])
+            tokens = BANK if b in (0, BLOCKS - 1) else N
+            for q in range(N // tokens):
+                piece = slice(q * tokens, (q + 1) * tokens)
+                looked_up = tables[b][:].indirect(offsets[:, q * (tokens // 16) : (q + 1) * (tokens // 16)])
                 nc.vector.tensor_tensor(summed[:, piece], looked_up, pos[:, piece], ADD)
                 if b == BLOCKS - 1:
                     nc.sync.dma_start(out[b * P : (b + 1) * P, piece], summed[:, piece])

@@ -5,14 +5,17 @@ BF16 = mybir.dt.bfloat16
 U16 = mybir.dt.uint16
 ADD = mybir.AluOpType.add
 SUBTRACT = mybir.AluOpType.subtract
-MULT = mybir.AluOpType.mult
+IS_EQUAL = mybir.AluOpType.is_equal
+NOT_EQUAL = mybir.AluOpType.not_equal
 COPY = mybir.ActivationFunctionType.Copy
+RELU = mybir.ActivationFunctionType.Relu
 
 P = 128
 C, S, N = 512, 4096, 2048
 BLOCKS = C // P
 BANK = 512
 BANKS = N // BANK
+TOP = 64
 COPIES = 4
 ROWS = 2 * COPIES
 
@@ -31,25 +34,36 @@ def tile_gridembedding_kernel(tc, emb, row, col, mask, row_vec, col_vec, offs, o
         nc.sync.dma_start(offsets[:], offs)
 
         vecs = held.tile([ROWS, C], F32, name="vecs")
-        grid = held.tile([ROWS, N], F32, name="grid")
-        inside = held.tile([ROWS, N], F32, name="inside")
         vecs_by_term = vecs[:].rearrange("(t w) c -> t w c", w=2)
-        grid_by_term = grid[:].rearrange("(t w) n -> t w n", w=2)
         nc.sync.dma_start(vecs_by_term[:, 0, :], row_vec.rearrange("c o -> o c").broadcast_to([COPIES, C]))
         nc.sync.dma_start(vecs_by_term[:, 1, :], col_vec.rearrange("c o -> o c").broadcast_to([COPIES, C]))
-        nc.sync.dma_start(grid_by_term[:, 0, :], row.broadcast_to([COPIES, N]))
-        nc.sync.dma_start(grid_by_term[:, 1, :], col.broadcast_to([COPIES, N]))
-        nc.sync.dma_start(inside[:], mask.broadcast_to([ROWS, N]))
+        raw = held.tile([3, N], F32, name="raw")
+        nc.sync.dma_start(raw[0:1, :], row)
+        nc.sync.dma_start(raw[1:2, :], col)
+        nc.sync.dma_start(raw[2:3, :], mask)
 
         tables = [held.tile([P, S], F32, name=f"table{b}") for b in range(BLOCKS)]
         for b in range(BLOCKS):
             nc.sync.dma_start(tables[b][:], emb[b * P : (b + 1) * P, :])
 
+        spread = held.tile([3, P], BF16, name="spread")
+        nc.gpsimd.memset(spread[:], 1.0)
+        nc.gpsimd.affine_select(
+            spread[:], spread[:], [[0, P // 2], [1, 2]], IS_EQUAL, 0.0, base=0, channel_multiplier=-1
+        )
+        nc.gpsimd.affine_select(
+            spread[:], spread[:], [[0, P]], NOT_EQUAL, float(TOP), base=-2, channel_multiplier=1
+        )
+
+        raw16 = held.tile([3, N], BF16, name="raw16")
         ab = held.tile([ROWS, N], BF16, name="ab")
 
         def make_ab(k):
             bank = slice(k * BANK, (k + 1) * BANK)
-            nc.vector.scalar_tensor_tensor(ab[:, bank], grid[:, bank], 1.0, inside[:, bank], ADD, MULT)
+            nc.vector.tensor_copy(raw16[:, bank], raw[:, bank])
+            lifted = psum.tile([P, BANK], F32, name="lifted")
+            nc.tensor.matmul(lifted[:], spread[:], raw16[:, bank], start=True, stop=True)
+            nc.scalar.activation(ab[:, bank], lifted[0:ROWS, :], RELU, bias=float(1 - TOP))
 
         terms = held.tile([ROWS, C], BF16, name="terms")
         rest = held.tile([4, C], F32, name="rest")

@@ -5,8 +5,6 @@ BF16 = mybir.dt.bfloat16
 U16 = mybir.dt.uint16
 ADD = mybir.AluOpType.add
 SUBTRACT = mybir.AluOpType.subtract
-IS_EQUAL = mybir.AluOpType.is_equal
-NOT_EQUAL = mybir.AluOpType.not_equal
 COPY = mybir.ActivationFunctionType.Copy
 RELU = mybir.ActivationFunctionType.Relu
 
@@ -30,9 +28,6 @@ def tile_gridembedding_kernel(tc, emb, row, col, mask, row_vec, col_vec, offs, o
         tc.tile_pool(name="blocks", bufs=BLOCKS) as blocks,
         tc.psum_pool(name="psum", bufs=4) as psum,
     ):
-        offsets = held.tile([P, N // 16], U16, name="offsets")
-        nc.sync.dma_start(offsets[:], offs)
-
         vecs = held.tile([ROWS, C], F32, name="vecs")
         vecs_by_term = vecs[:].rearrange("(t w) c -> t w c", w=2)
         nc.sync.dma_start(vecs_by_term[:, 0, :], row_vec.rearrange("c o -> o c").broadcast_to([COPIES, C]))
@@ -42,49 +37,57 @@ def tile_gridembedding_kernel(tc, emb, row, col, mask, row_vec, col_vec, offs, o
         nc.sync.dma_start(raw[1:2, :], col)
         nc.sync.dma_start(raw[2:3, :], mask)
 
+        offsets = held.tile([P, N // 16], U16, name="offsets")
+        nc.sync.dma_start(offsets[:], offs)
+
         tables = [held.tile([P, S], F32, name=f"table{b}") for b in range(BLOCKS)]
         for b in range(BLOCKS):
             nc.sync.dma_start(tables[b][:], emb[b * P : (b + 1) * P, :])
 
         spread = held.tile([3, P], BF16, name="spread")
-        nc.gpsimd.memset(spread[:], 1.0)
-        nc.gpsimd.affine_select(
-            spread[:], spread[:], [[0, P // 2], [1, 2]], IS_EQUAL, 0.0, base=0, channel_multiplier=-1
-        )
-        nc.gpsimd.affine_select(
-            spread[:], spread[:], [[0, P]], NOT_EQUAL, float(TOP), base=-2, channel_multiplier=1
-        )
+        spread_pairs = spread[:].rearrange("p (m w) -> p m w", w=2)
+        nc.vector.memset(spread[:], float(TOP))
+        nc.vector.memset(spread_pairs[0:2, :, 0], 0.0)
+        nc.vector.memset(spread_pairs[0:2, :, 1], 1.0)
+        nc.vector.memset(spread_pairs[0:1, :, 0], 1.0)
+        nc.vector.memset(spread_pairs[0:1, :, 1], 0.0)
 
-        raw16 = held.tile([3, N], BF16, name="raw16")
+        terms = held.tile([ROWS, C], BF16, name="terms")
+        rest = held.tile([4, C], F32, name="rest")
+        nc.vector.memset(terms[:], 0.0)
+        runs = (slice(0, P), slice(P, C))
+        for run in runs:
+            nc.vector.tensor_copy(terms[0:6, run], vecs[0:6, run])
+        for run in runs:
+            nc.vector.tensor_tensor(rest[0:4, run], vecs[0:4, run], terms[0:4, run], SUBTRACT)
+        for run in runs:
+            nc.vector.tensor_copy(terms[0:4, run], rest[0:4, run])
+        for run in runs:
+            nc.vector.tensor_tensor(terms[0:2, run], rest[0:2, run], terms[0:2, run], SUBTRACT)
+
+        upper = raw[:].bitcast(BF16).rearrange("p (n h) -> p n h", h=2)[:, :, 1]
         ab = held.tile([ROWS, N], BF16, name="ab")
 
         def make_ab(k):
             bank = slice(k * BANK, (k + 1) * BANK)
-            nc.vector.tensor_copy(raw16[:, bank], raw[:, bank])
             lifted = psum.tile([P, BANK], F32, name="lifted")
-            nc.tensor.matmul(lifted[:], spread[:], raw16[:, bank], start=True, stop=True)
+            nc.tensor.matmul(lifted[:], spread[:], upper[:, bank], start=True, stop=True)
             nc.scalar.activation(ab[:, bank], lifted[0:ROWS, :], RELU, bias=float(1 - TOP))
 
-        terms = held.tile([ROWS, C], BF16, name="terms")
-        rest = held.tile([4, C], F32, name="rest")
-        nc.gpsimd.memset(terms[:], 0.0)
-        nc.vector.tensor_copy(terms[0:6, :], vecs[0:6, :])
-        make_ab(0)
-        nc.vector.tensor_tensor(rest[0:4, :], vecs[0:4, :], terms[0:4, :], SUBTRACT)
-        make_ab(1)
-        nc.vector.tensor_copy(terms[0:4, :], rest[0:4, :])
-        make_ab(2)
-        nc.vector.tensor_tensor(terms[0:2, :], rest[0:2, :], terms[0:2, :], SUBTRACT)
-        make_ab(3)
+        def make_pos(pos, b, k):
+            bank = slice(k * BANK, (k + 1) * BANK)
+            pos_bank = psum.tile([P, BANK], F32, name="pos_bank")
+            nc.tensor.matmul(pos_bank[:], terms[:, b * P : (b + 1) * P], ab[:, bank], start=True, stop=True)
+            nc.scalar.activation(pos[:, bank], pos_bank[:], COPY)
 
+        make_ab(0)
         for b in range(BLOCKS):
             pos = blocks.tile([P, N], F32, name="pos")
             summed = blocks.tile([P, N], F32, name="summed")
             for k in range(BANKS):
-                bank = slice(k * BANK, (k + 1) * BANK)
-                pos_bank = psum.tile([P, BANK], F32, name="pos_bank")
-                nc.tensor.matmul(pos_bank[:], terms[:, b * P : (b + 1) * P], ab[:, bank], start=True, stop=True)
-                nc.scalar.activation(pos[:, bank], pos_bank[:], COPY)
+                if b == 0 and k + 1 < BANKS:
+                    make_ab(k + 1)
+                make_pos(pos, b, k)
             tokens = BANK if b in (0, BLOCKS - 1) else N
             for q in range(N // tokens):
                 piece = slice(q * tokens, (q + 1) * tokens)

@@ -17,8 +17,15 @@ TOP = 64
 COPIES = 4
 ROWS = 2 * COPIES
 
+HEAD_STEPS = 2
+TAIL_STEPS = 3
+
 FLOPS = 4 * C * N
 BYTES = 4 * (2 * C * N + 3 * N + 2 * C) + 2 * P * (N // 16)
+
+
+def halves(total, steps):
+    return [total >> (i + 1) for i in range(steps)] + [total >> steps]
 
 
 def tile_gridembedding_kernel(tc, emb, row, col, mask, row_vec, col_vec, offs, out):
@@ -88,12 +95,19 @@ def tile_gridembedding_kernel(tc, emb, row, col, mask, row_vec, col_vec, offs, o
                 if b == 0 and k + 1 < BANKS:
                     make_ab(k + 1)
                 make_pos(pos, b, k)
-            tokens = BANK if b in (0, BLOCKS - 1) else N
-            for q in range(N // tokens):
-                piece = slice(q * tokens, (q + 1) * tokens)
-                looked_up = tables[b][:].indirect(offsets[:, q * (tokens // 16) : (q + 1) * (tokens // 16)])
+            if b == 0:
+                widths = list(reversed(halves(N, HEAD_STEPS)))
+            elif b == BLOCKS - 1:
+                widths = halves(N, TAIL_STEPS)
+            else:
+                widths = [N]
+            first = 0
+            for width in widths:
+                piece = slice(first, first + width)
+                looked_up = tables[b][:].indirect(offsets[:, first // 16 : (first + width) // 16])
                 nc.vector.tensor_tensor(summed[:, piece], looked_up, pos[:, piece], ADD)
                 if b == BLOCKS - 1:
                     nc.sync.dma_start(out[b * P : (b + 1) * P, piece], summed[:, piece])
+                first += width
             if b < BLOCKS - 1:
                 nc.sync.dma_start(out[b * P : (b + 1) * P, :], summed[:])

@@ -18,7 +18,7 @@ COPIES = 4
 ROWS = 2 * COPIES
 
 HEAD_STEPS = 2
-TAIL_STEPS = 3
+TAIL_STEPS = 2
 
 FLOPS = 4 * C * N
 BYTES = 4 * (2 * C * N + 3 * N + 2 * C) + 2 * P * (N // 16)
@@ -35,6 +35,9 @@ def tile_gridembedding_kernel(tc, emb, row, col, mask, row_vec, col_vec, offs, o
         tc.tile_pool(name="blocks", bufs=BLOCKS) as blocks,
         tc.psum_pool(name="psum", bufs=4) as psum,
     ):
+        emb_blocks = emb.rearrange("(p b) s -> p b s", b=BLOCKS)
+        out_rows = out.rearrange("(p b) n -> p (b n)", b=BLOCKS)
+
         vecs = held.tile([ROWS, C], F32, name="vecs")
         vecs_by_term = vecs[:].rearrange("(t w) c -> t w c", w=2)
         nc.sync.dma_start(vecs_by_term[:, 0, :], row_vec.rearrange("c o -> o c").broadcast_to([COPIES, C]))
@@ -49,7 +52,7 @@ def tile_gridembedding_kernel(tc, emb, row, col, mask, row_vec, col_vec, offs, o
 
         tables = [held.tile([P, S], F32, name=f"table{b}") for b in range(BLOCKS)]
         for b in range(BLOCKS):
-            nc.sync.dma_start(tables[b][:], emb[b * P : (b + 1) * P, :])
+            nc.sync.dma_start(tables[b][:], emb_blocks[:, b, :])
 
         spread = held.tile([3, P], BF16, name="spread")
         spread_pairs = spread[:].rearrange("p (m w) -> p m w", w=2)
@@ -62,15 +65,11 @@ def tile_gridembedding_kernel(tc, emb, row, col, mask, row_vec, col_vec, offs, o
         terms = held.tile([ROWS, C], BF16, name="terms")
         rest = held.tile([4, C], F32, name="rest")
         nc.vector.memset(terms[:], 0.0)
-        runs = (slice(0, P), slice(P, C))
-        for run in runs:
-            nc.vector.tensor_copy(terms[0:6, run], vecs[0:6, run])
-        for run in runs:
-            nc.vector.tensor_tensor(rest[0:4, run], vecs[0:4, run], terms[0:4, run], SUBTRACT)
-        for run in runs:
-            nc.vector.tensor_copy(terms[0:4, run], rest[0:4, run])
-        for run in runs:
-            nc.vector.tensor_tensor(terms[0:2, run], rest[0:2, run], terms[0:2, run], SUBTRACT)
+        nc.vector.tensor_copy(terms[0:6, :], vecs[0:6, :])
+        nc.vector.tensor_tensor(rest[0:4, :], vecs[0:4, :], terms[0:4, :], SUBTRACT)
+        nc.vector.tensor_copy(terms[0:4, :], rest[0:4, :])
+        nc.vector.tensor_tensor(terms[0:2, :], rest[0:2, :], terms[0:2, :], SUBTRACT)
+        terms_blocks = terms[:].rearrange("r (p b) -> r b p", b=BLOCKS)
 
         upper = raw[:].bitcast(BF16).rearrange("p (n h) -> p n h", h=2)[:, :, 1]
         ab = held.tile([ROWS, N], BF16, name="ab")
@@ -84,13 +83,14 @@ def tile_gridembedding_kernel(tc, emb, row, col, mask, row_vec, col_vec, offs, o
         def make_pos(pos, b, k):
             bank = slice(k * BANK, (k + 1) * BANK)
             pos_bank = psum.tile([P, BANK], F32, name="pos_bank")
-            nc.tensor.matmul(pos_bank[:], terms[:, b * P : (b + 1) * P], ab[:, bank], start=True, stop=True)
+            nc.tensor.matmul(pos_bank[:], terms_blocks[:, b, :], ab[:, bank], start=True, stop=True)
             nc.scalar.activation(pos[:, bank], pos_bank[:], COPY)
 
+        summed = held.tile([P, BLOCKS * N], F32, name="summed")
+        stored = 0
         make_ab(0)
         for b in range(BLOCKS):
             pos = blocks.tile([P, N], F32, name="pos")
-            summed = blocks.tile([P, N], F32, name="summed")
             for k in range(BANKS):
                 if b == 0 and k + 1 < BANKS:
                     make_ab(k + 1)
@@ -105,9 +105,9 @@ def tile_gridembedding_kernel(tc, emb, row, col, mask, row_vec, col_vec, offs, o
             for width in widths:
                 piece = slice(first, first + width)
                 looked_up = tables[b][:].indirect(offsets[:, first // 16 : (first + width) // 16])
-                nc.vector.tensor_tensor(summed[:, piece], looked_up, pos[:, piece], ADD)
-                if b == BLOCKS - 1:
-                    nc.sync.dma_start(out[b * P : (b + 1) * P, piece], summed[:, piece])
+                nc.vector.tensor_tensor(summed[:, b * N + first : b * N + first + width], looked_up, pos[:, piece], ADD)
                 first += width
-            if b < BLOCKS - 1:
-                nc.sync.dma_start(out[b * P : (b + 1) * P, :], summed[:])
+                summed_so_far = b * N + first
+                if b == BLOCKS - 1 or (b > 0 and first == N):
+                    nc.sync.dma_start(out_rows[:, stored:summed_so_far], summed[:, stored:summed_so_far])
+                    stored = summed_so_far

@@ -5,6 +5,7 @@ BF16 = mybir.dt.bfloat16
 U16 = mybir.dt.uint16
 ADD = mybir.AluOpType.add
 SUBTRACT = mybir.AluOpType.subtract
+MAX = mybir.AluOpType.max
 COPY = mybir.ActivationFunctionType.Copy
 RELU = mybir.ActivationFunctionType.Relu
 
@@ -14,6 +15,7 @@ BLOCKS = C // P
 BANK = 512
 BANKS = N // BANK
 TOP = 64
+TERMS = 3
 COPIES = 4
 ROWS = 2 * COPIES
 
@@ -38,14 +40,14 @@ def tile_gridembedding_kernel(tc, emb, row, col, mask, row_vec, col_vec, offs, o
         emb_blocks = emb.rearrange("(p b) s -> p b s", b=BLOCKS)
         out_rows = out.rearrange("(p b) n -> p (b n)", b=BLOCKS)
 
-        vecs = held.tile([ROWS, C], F32, name="vecs")
-        vecs_by_term = vecs[:].rearrange("(t w) c -> t w c", w=2)
-        nc.sync.dma_start(vecs_by_term[:, 0, :], row_vec.rearrange("c o -> o c").broadcast_to([COPIES, C]))
-        nc.sync.dma_start(vecs_by_term[:, 1, :], col_vec.rearrange("c o -> o c").broadcast_to([COPIES, C]))
         raw = held.tile([3, N], F32, name="raw")
         nc.sync.dma_start(raw[0:1, :], row)
         nc.sync.dma_start(raw[1:2, :], col)
         nc.sync.dma_start(raw[2:3, :], mask)
+        vecs = held.tile([ROWS, C], F32, name="vecs")
+        vecs_by_term = vecs[:].rearrange("(t w) c -> t w c", w=2)
+        nc.scalar.dma_start(vecs_by_term[:, 0, :], row_vec.rearrange("c o -> o c").broadcast_to([COPIES, C]))
+        nc.scalar.dma_start(vecs_by_term[:, 1, :], col_vec.rearrange("c o -> o c").broadcast_to([COPIES, C]))
 
         offsets = held.tile([P, N // 16], U16, name="offsets")
         nc.sync.dma_start(offsets[:], offs)
@@ -55,21 +57,18 @@ def tile_gridembedding_kernel(tc, emb, row, col, mask, row_vec, col_vec, offs, o
             nc.sync.dma_start(tables[b][:], emb_blocks[:, b, :])
 
         spread = held.tile([3, P], BF16, name="spread")
-        spread_pairs = spread[:].rearrange("p (m w) -> p m w", w=2)
-        nc.vector.memset(spread[:], float(TOP))
+        nc.vector.memset(spread[:], 0.0)
+        spread_pairs = spread[:, 0 : 2 * TERMS].rearrange("p (m w) -> p m w", w=2)
+        nc.vector.memset(spread_pairs[0:3, :, :], float(TOP))
         nc.vector.memset(spread_pairs[0:2, :, 0], 0.0)
         nc.vector.memset(spread_pairs[0:2, :, 1], 1.0)
         nc.vector.memset(spread_pairs[0:1, :, 0], 1.0)
         nc.vector.memset(spread_pairs[0:1, :, 1], 0.0)
 
-        terms = held.tile([ROWS, C], BF16, name="terms")
-        rest = held.tile([4, C], F32, name="rest")
-        nc.vector.memset(terms[:], 0.0)
-        nc.vector.tensor_copy(terms[0:6, :], vecs[0:6, :])
-        nc.vector.tensor_tensor(rest[0:4, :], vecs[0:4, :], terms[0:4, :], SUBTRACT)
-        nc.vector.tensor_copy(terms[0:4, :], rest[0:4, :])
-        nc.vector.tensor_tensor(terms[0:2, :], rest[0:2, :], terms[0:2, :], SUBTRACT)
-        terms_blocks = terms[:].rearrange("r (p b) -> r b p", b=BLOCKS)
+        vecs_upper = vecs[:].bitcast(BF16).rearrange("r (c h) -> r c h", h=2)[:, :, 1]
+        nc.vector.tensor_tensor(vecs[0:4, :], vecs[0:4, :], vecs_upper[0:4, :], SUBTRACT)
+        nc.vector.tensor_tensor(vecs[0:2, :], vecs[0:2, :], vecs_upper[0:2, :], SUBTRACT)
+        terms_blocks = vecs_upper.rearrange("r (p b) -> r b p", b=BLOCKS)
 
         upper = raw[:].bitcast(BF16).rearrange("p (n h) -> p n h", h=2)[:, :, 1]
         ab = held.tile([ROWS, N], BF16, name="ab")
@@ -78,7 +77,10 @@ def tile_gridembedding_kernel(tc, emb, row, col, mask, row_vec, col_vec, offs, o
             bank = slice(k * BANK, (k + 1) * BANK)
             lifted = psum.tile([P, BANK], F32, name="lifted")
             nc.tensor.matmul(lifted[:], spread[:], upper[:, bank], start=True, stop=True)
-            nc.scalar.activation(ab[:, bank], lifted[0:ROWS, :], RELU, bias=float(1 - TOP))
+            if k % 2 == 0:
+                nc.scalar.activation(ab[:, bank], lifted[0:ROWS, :], RELU, bias=float(1 - TOP))
+            else:
+                nc.vector.tensor_scalar(ab[:, bank], lifted[0:ROWS, :], float(1 - TOP), 0.0, ADD, MAX)
 
         def make_pos(pos, b, k):
             bank = slice(k * BANK, (k + 1) * BANK)

@@ -20,7 +20,7 @@ COPIES = 4
 ROWS = 2 * COPIES
 
 HEAD_STEPS = 2
-TAIL_STEPS = 2
+TAIL = [N // 4, N // 8]
 
 FLOPS = 4 * C * N
 BYTES = 4 * (2 * C * N + 3 * N + 2 * C) + 2 * P * (N // 16)
@@ -100,7 +100,7 @@ def tile_gridembedding_kernel(tc, emb, row, col, mask, row_vec, col_vec, offs, o
             if b == 0:
                 widths = list(reversed(halves(N, HEAD_STEPS)))
             elif b == BLOCKS - 1:
-                widths = halves(N, TAIL_STEPS)
+                widths = [N - sum(TAIL)] + TAIL
             else:
                 widths = [N]
             first = 0

import concourse.mybir as mybir

F32 = mybir.dt.float32
BF16 = mybir.dt.bfloat16
U16 = mybir.dt.uint16
ADD = mybir.AluOpType.add
SUBTRACT = mybir.AluOpType.subtract
MAX = mybir.AluOpType.max
COPY = mybir.ActivationFunctionType.Copy
RELU = mybir.ActivationFunctionType.Relu

P = 128
C, S, N = 512, 4096, 2048
BLOCKS = C // P
BANK = 512
BANKS = N // BANK
TOP = 64
TERMS = 3
COPIES = 4
ROWS = 2 * COPIES

HEAD_STEPS = 2
TAIL = [N // 4, N // 8]

FLOPS = 4 * C * N
BYTES = 4 * (2 * C * N + 3 * N + 2 * C) + 2 * P * (N // 16)


def halves(total, steps):
    return [total >> (i + 1) for i in range(steps)] + [total >> steps]


def tile_gridembedding_kernel(tc, emb, row, col, mask, row_vec, col_vec, offs, out):
    nc = tc.nc
    with (
        tc.tile_pool(name="held", bufs=1) as held,
        tc.tile_pool(name="blocks", bufs=BLOCKS) as blocks,
        tc.psum_pool(name="psum", bufs=4) as psum,
    ):
        emb_blocks = emb.rearrange("(p b) s -> p b s", b=BLOCKS)
        out_rows = out.rearrange("(p b) n -> p (b n)", b=BLOCKS)

        raw = held.tile([3, N], F32, name="raw")
        nc.sync.dma_start(raw[0:1, :], row)
        nc.sync.dma_start(raw[1:2, :], col)
        nc.sync.dma_start(raw[2:3, :], mask)
        vecs = held.tile([ROWS, C], F32, name="vecs")
        vecs_by_term = vecs[:].rearrange("(t w) c -> t w c", w=2)
        nc.scalar.dma_start(vecs_by_term[:, 0, :], row_vec.rearrange("c o -> o c").broadcast_to([COPIES, C]))
        nc.scalar.dma_start(vecs_by_term[:, 1, :], col_vec.rearrange("c o -> o c").broadcast_to([COPIES, C]))

        offsets = held.tile([P, N // 16], U16, name="offsets")
        nc.sync.dma_start(offsets[:], offs)

        tables = [held.tile([P, S], F32, name=f"table{b}") for b in range(BLOCKS)]
        for b in range(BLOCKS):
            nc.sync.dma_start(tables[b][:], emb_blocks[:, b, :])

        spread = held.tile([3, P], BF16, name="spread")
        nc.vector.memset(spread[:], 0.0)
        spread_pairs = spread[:, 0 : 2 * TERMS].rearrange("p (m w) -> p m w", w=2)
        nc.vector.memset(spread_pairs[0:3, :, :], float(TOP))
        nc.vector.memset(spread_pairs[0:2, :, 0], 0.0)
        nc.vector.memset(spread_pairs[0:2, :, 1], 1.0)
        nc.vector.memset(spread_pairs[0:1, :, 0], 1.0)
        nc.vector.memset(spread_pairs[0:1, :, 1], 0.0)

        vecs_upper = vecs[:].bitcast(BF16).rearrange("r (c h) -> r c h", h=2)[:, :, 1]
        nc.vector.tensor_tensor(vecs[0:4, :], vecs[0:4, :], vecs_upper[0:4, :], SUBTRACT)
        nc.vector.tensor_tensor(vecs[0:2, :], vecs[0:2, :], vecs_upper[0:2, :], SUBTRACT)
        terms_blocks = vecs_upper.rearrange("r (p b) -> r b p", b=BLOCKS)

        upper = raw[:].bitcast(BF16).rearrange("p (n h) -> p n h", h=2)[:, :, 1]
        ab = held.tile([ROWS, N], BF16, name="ab")

        def make_ab(k):
            bank = slice(k * BANK, (k + 1) * BANK)
            lifted = psum.tile([P, BANK], F32, name="lifted")
            nc.tensor.matmul(lifted[:], spread[:], upper[:, bank], start=True, stop=True)
            if k % 2 == 0:
                nc.scalar.activation(ab[:, bank], lifted[0:ROWS, :], RELU, bias=float(1 - TOP))
            else:
                nc.vector.tensor_scalar(ab[:, bank], lifted[0:ROWS, :], float(1 - TOP), 0.0, ADD, MAX)

        def make_pos(pos, b, k):
            bank = slice(k * BANK, (k + 1) * BANK)
            pos_bank = psum.tile([P, BANK], F32, name="pos_bank")
            nc.tensor.matmul(pos_bank[:], terms_blocks[:, b, :], ab[:, bank], start=True, stop=True)
            nc.scalar.activation(pos[:, bank], pos_bank[:], COPY)

        summed = held.tile([P, BLOCKS * N], F32, name="summed")
        stored = 0
        make_ab(0)
        for b in range(BLOCKS):
            pos = blocks.tile([P, N], F32, name="pos")
            for k in range(BANKS):
                if b == 0 and k + 1 < BANKS:
                    make_ab(k + 1)
                make_pos(pos, b, k)
            if b == 0:
                widths = list(reversed(halves(N, HEAD_STEPS)))
            elif b == BLOCKS - 1:
                widths = [N - sum(TAIL)] + TAIL
            else:
                widths = [N]
            first = 0
            for width in widths:
                piece = slice(first, first + width)
                looked_up = tables[b][:].indirect(offsets[:, first // 16 : (first + width) // 16])
                nc.vector.tensor_tensor(summed[:, b * N + first : b * N + first + width], looked_up, pos[:, piece], ADD)
                first += width
                summed_so_far = b * N + first
                if b == BLOCKS - 1 or (b > 0 and first == N):
                    nc.sync.dma_start(out_rows[:, stored:summed_so_far], summed[:, stored:summed_so_far])
                    stored = summed_so_far
